import numpy as np
import ml_dtypes


def mxq(x, axis, fmt="e4m3"):
    dtype, down = {"e4m3": (ml_dtypes.float8_e4m3fn, 7), "e5m2": (ml_dtypes.float8_e5m2, 14)}[fmt]
    v = np.moveaxis(np.asarray(x, np.float32).astype(ml_dtypes.bfloat16).astype(np.float64), axis, -1)
    blocks = v.reshape(v.shape[:-1] + (-1, 32))
    amax = np.abs(blocks).max(-1, keepdims=True)
    byte = np.maximum(np.where(amax > 0, np.frexp(amax)[1] - 1 + 127, 0) - down, 1)
    scale = np.exp2(byte - 127.0)
    codes = (blocks / scale).astype(np.float32).astype(dtype).astype(np.float64)
    return np.moveaxis((codes * scale).reshape(v.shape), -1, axis)


WIDE = False


def mx_kscale(k):
    if not WIDE:
        return np.ones(k)
    levels = np.array([10, -10, 5, -5, 0])
    a = np.random.permutation(np.resize(levels, k // 512 * 4)).reshape(k // 512, 4)
    idx = np.arange(k)
    return np.exp2(a[idx // 512, idx % 128 // 32])


BF16 = ml_dtypes.bfloat16


def bf(x):
    return np.asarray(x, np.float32).astype(BF16)


def f64(x):
    return np.asarray(x).astype(np.float64)


M, K, N = 16384, 512, 128
BLOCK = 128


def setup_inputs():
    s = mx_kscale(K)
    return {"x": bf(np.random.standard_normal((M, K)) * s),
            "weight": bf(np.random.standard_normal((N, K)) / np.sqrt(K) / s[None, :]),
            "weight_scale_inv": bf(np.random.uniform(0.5, 1.5, (N // BLOCK, K // BLOCK))),
            "bias": bf(np.random.standard_normal(N) * 0.3)}


def reference(x, weight, weight_scale_inv, bias):
    n, k = weight.shape
    nb, kb = weight_scale_inv.shape
    w_deq = (f64(weight).reshape(nb, BLOCK, kb, BLOCK) * f64(weight_scale_inv)[:, None, :, None]).reshape(n, k)
    out = mxq(f64(x), 1, "e4m3") @ mxq(w_deq, 1, "e4m3").T
    return out + f64(bias)[None, :]

@@ -1,0 +1,178 @@
+from contextlib import ExitStack
+
+import concourse.mybir as mybir
+from concourse.masks import make_identity
+
+F32 = mybir.dt.float32
+BF16 = mybir.dt.bfloat16
+U32 = mybir.dt.uint32
+U8 = mybir.dt.uint8
+FP8X4 = mybir.dt.float8_e4m3fn_x4
+MULT = mybir.AluOpType.mult
+ADD = mybir.AluOpType.add
+
+P = 128
+M, K, N = 16384, 512, 128
+FLOPS = 2 * M * K * N
+
+UNIT = 4
+CHUNKS = [4, 4, 8, 16, 16, 16, 16, 16, 16, 16]
+BIG = 16
+
+
+def tile_fp8columnparallellinear_t_kernel(tc, x, weight, weight_scale_inv, bias, out):
+    nc = tc.nc
+    assert sum(CHUNKS) * P == M
+    with ExitStack() as ctx:
+        const = ctx.enter_context(tc.tile_pool(name="const", bufs=1))
+        xpool = ctx.enter_context(tc.tile_pool(name="xin", bufs=1))
+        opool = ctx.enter_context(tc.tile_pool(name="res", bufs=1))
+        gpool = ctx.enter_context(tc.tile_pool(name="grouped", bufs=4))
+        qpool = ctx.enter_context(tc.tile_pool(name="quant", bufs=4))
+        ps_t = ctx.enter_context(tc.psum_pool(name="pst", bufs=5))
+        ps_o = ctx.enter_context(tc.psum_pool(name="pso", bufs=3))
+        ctx.enter_context(tc.manual_schedule())
+
+        w_sb = const.tile([P, K], BF16, name="w_sb")
+        row = const.tile([P, 256], BF16, name="row")
+        nc.vector.memset(row[:], 0.0)
+        x_tiles = []
+        o_tiles = []
+        o_views = []
+        r0 = 0
+        for c, tiles in enumerate(CHUNKS):
+            rows = tiles * P
+            if tiles == BIG:
+                xt = xpool.tile([P, tiles * K], BF16, name="xbig%d" % c, tag="xbig", bufs=6)
+            else:
+                xt = xpool.tile([P, tiles * K], BF16, name="xsmall%d" % c)
+            nc.sync.dma_start(out=xt[:], in_=x[r0 : r0 + rows, :].rearrange("(p t) k -> p (t k)", t=tiles))
+            if c == 0:
+                nc.sync.dma_start(out=w_sb[:], in_=weight)
+                nc.sync.dma_start(out=row[0:1, 0:N], in_=bias.rearrange("(o n) -> o n", o=1))
+                nc.sync.dma_start(out=row[0:1, N : N + 4], in_=weight_scale_inv)
+            x_tiles.append(xt)
+            ot = opool.tile([P, tiles, N], F32, name="o%d" % c)
+            o_tiles.append(ot)
+            o_views.append(out[r0 : r0 + rows, :].rearrange("(p t) n -> p t n", t=tiles))
+            r0 += rows
+
+        ident_f = const.tile([P, P], F32, name="ident_f")
+        make_identity(nc, ident_f[:])
+        ident_b = const.tile([P, P], BF16, name="ident_b")
+        make_identity(nc, ident_b[:])
+        ones = const.tile([P, P], BF16, name="ones")
+        nc.vector.memset(ones[:], 1.0)
+        w_codes = const.tile([P, N], U32, name="w_codes", align_bytes=64)
+        w_scales = const.tile([P, N], U8, name="w_scales", align_bytes=64)
+        bias4 = const.tile([P, UNIT, N], F32, name="bias4")
+
+        def prepare_weight():
+            ps_c = ps_o.tile([P, 256], F32, name="ps_c", tag="O")
+            nc.tensor.matmul(out=ps_c[:], lhsT=ones[:], rhs=row[:], start=True, stop=True)
+            scale_sb = const.tile([P, 4], F32, name="scale_sb")
+            nc.vector.tensor_copy(out=scale_sb[:], in_=ps_c[:, N : N + 4])
+            wd = const.tile([P, 4, P], BF16, name="wd")
+            for j in range(4):
+                u, h = divmod(j, 2)
+                nc.vector.tensor_scalar(
+                    out=wd[:, 2 * u : 2 * u + 2, 64 * h : 64 * h + 64],
+                    in0=w_sb[:, P * j : P * j + P].rearrange("n (q e) -> n e q", e=2),
+                    scalar1=scale_sb[:, j : j + 1],
+                    scalar2=None,
+                    op0=MULT,
+                )
+            pw = ps_t.tile([P, 4, P], BF16, name="pw", tag="T")
+            for t in range(4):
+                nc.tensor.transpose(pw[:, t, :], wd[:, t, :], ident_b[:])
+            nc.vector.tensor_copy(out=bias4[:], in_=ps_c[:, 0:N].unsqueeze(1).to_broadcast([P, UNIT, N]))
+            wg = const.tile([P, N, 4], BF16, name="wg", align_bytes=64)
+            nc.vector.tensor_copy(out=wg[:], in_=pw[:].rearrange("p t n -> p n t"))
+            nc.vector.quantize_mx(
+                out=w_codes[:].bitcast(FP8X4), scales=w_scales[:], in_=wg[:].rearrange("p n t -> p (n t)")
+            )
+
+        units = []
+        for c, tiles in enumerate(CHUNKS):
+            for t0 in range(0, tiles, UNIT):
+                units.append((c, t0))
+        n_units = len(units)
+        store_from = {}
+        for c, tiles in enumerate(CHUNKS):
+            store_from[(c, tiles)] = 0
+        last = len(CHUNKS) - 1
+        store_from[(last, 8)] = 0
+        store_from[(last, 12)] = 8
+        store_from[(last, 16)] = 12
+        banks = {}
+        grouped = {}
+        quant = {}
+        sums = {}
+
+        def transposes(s):
+            c, t0 = units[s]
+            xf = x_tiles[c][:].bitcast(F32)
+            pair = []
+            for b in range(2):
+                pt = ps_t.tile([P, 2, 256], F32, name="pt%d_%d" % (s, b), tag="T")
+                for jj in range(2):
+                    t = t0 + 2 * b + jj
+                    for u in range(2):
+                        nc.tensor.transpose(
+                            pt[:, u, P * jj : P * jj + P],
+                            xf[:, 256 * t + P * u : 256 * t + P * u + P],
+                            ident_f[:],
+                        )
+                pair.append(pt)
+            banks[s] = pair
+
+        def copies(s):
+            g = gpool.tile([P, UNIT * P * 4], BF16, name="g%d" % s, tag="g", align_bytes=64)
+            gf = g[:].bitcast(F32)
+            for b in range(2):
+                nc.scalar.copy(
+                    out=gf[:, 512 * b : 512 * b + 512].rearrange("p (c u) -> p c u", u=2),
+                    in_=banks[s][b][:].rearrange("p u c -> p c u"),
+                )
+            grouped[s] = g
+
+        def quantise(s):
+            codes = qpool.tile([P, UNIT * P], U32, name="codes%d" % s, tag="codes", align_bytes=64)
+            scales = qpool.tile([P, UNIT * P], U8, name="scales%d" % s, tag="scales", align_bytes=64)
+            nc.vector.quantize_mx(out=codes[:].bitcast(FP8X4), scales=scales[:], in_=grouped[s][:])
+            quant[s] = (codes, scales)
+
+        def passes(s):
+            codes, scales = quant[s]
+            po = ps_o.tile([P, UNIT, N], F32, name="po%d" % s, tag="O")
+            for j in range(UNIT):
+                nc.tensor.matmul_mx(
+                    out=po[:, j, :],
+                    lhsT=codes[:, P * j : P * j + P].bitcast(FP8X4),
+                    lhsT_scale=scales[:, P * j : P * j + P],
+                    rhs=w_codes[:].bitcast(FP8X4),
+                    rhs_scale=w_scales[:],
+                    start=True,
+                    stop=True,
+                )
+            sums[s] = po
+
+        def finish(s):
+            c, t0 = units[s]
+            nc.vector.tensor_tensor(out=o_tiles[c][:, t0 : t0 + UNIT, :], in0=sums[s][:], in1=bias4[:], op=ADD)
+            first = store_from.get((c, t0 + UNIT))
+            if first is not None:
+                nc.sync.dma_start(out=o_views[c][:, first : t0 + UNIT, :], in_=o_tiles[c][:, first : t0 + UNIT, :])
+
+        for s in range(n_units + 3):
+            if s < n_units:
+                transposes(s)
+                copies(s)
+            if s == 0:
+                prepare_weight()
+            if 0 <= s - 2 < n_units:
+                passes(s - 2)
+            if 0 <= s - 1 < n_units:
+                quantise(s - 1)
+            if 0 <= s - 3 < n_units:
+                finish(s - 3)

@@ -16,13 +16,15 @@ M, K, N = 16384, 512, 128
 FLOPS = 2 * M * K * N
 
 UNIT = 4
-CHUNKS = [4, 4, 8, 16, 16, 16, 16, 16, 16, 16]
+TILES = M // P
+LOADS = [4, 4, 8, 8, 8, 16, 16, 16, 16, 16, 16]
+STORES = [32, 32, 32, 16, 8, 8]
 BIG = 16
 
 
 def tile_fp8columnparallellinear_t_kernel(tc, x, weight, weight_scale_inv, bias, out):
     nc = tc.nc
-    assert sum(CHUNKS) * P == M
+    assert sum(LOADS) == TILES and sum(STORES) == TILES
     with ExitStack() as ctx:
         const = ctx.enter_context(tc.tile_pool(name="const", bufs=1))
         xpool = ctx.enter_context(tc.tile_pool(name="xin", bufs=1))
@@ -36,26 +38,31 @@ def tile_fp8columnparallellinear_t_kernel(tc, x, weight, weight_scale_inv, bias,
         w_sb = const.tile([P, K], BF16, name="w_sb")
         row = const.tile([P, 256], BF16, name="row")
         nc.vector.memset(row[:], 0.0)
-        x_tiles = []
-        o_tiles = []
-        o_views = []
-        r0 = 0
-        for c, tiles in enumerate(CHUNKS):
-            rows = tiles * P
+        x_view = x.rearrange("(p t) k -> p t k", t=TILES)
+        out_view = out.rearrange("(p t) n -> p t n", t=TILES)
+        x_of = []
+        first = 0
+        for c, tiles in enumerate(LOADS):
             if tiles == BIG:
-                xt = xpool.tile([P, tiles * K], BF16, name="xbig%d" % c, tag="xbig", bufs=6)
+                xt = xpool.tile([P, tiles, K], BF16, name="xbig%d" % c, tag="xbig", bufs=5)
             else:
-                xt = xpool.tile([P, tiles * K], BF16, name="xsmall%d" % c)
-            nc.sync.dma_start(out=xt[:], in_=x[r0 : r0 + rows, :].rearrange("(p t) k -> p (t k)", t=tiles))
+                xt = xpool.tile([P, tiles, K], BF16, name="xsmall%d" % c)
+            nc.sync.dma_start(out=xt[:], in_=x_view[:, first : first + tiles, :])
             if c == 0:
                 nc.sync.dma_start(out=w_sb[:], in_=weight)
                 nc.sync.dma_start(out=row[0:1, 0:N], in_=bias.rearrange("(o n) -> o n", o=1))
                 nc.sync.dma_start(out=row[0:1, N : N + 4], in_=weight_scale_inv)
-            x_tiles.append(xt)
+            xf = xt[:].rearrange("p t k -> p (t k)").bitcast(F32)
+            for t in range(tiles):
+                x_of.append((xf, t))
+            first += tiles
+        o_of = []
+        first = 0
+        for c, tiles in enumerate(STORES):
             ot = opool.tile([P, tiles, N], F32, name="o%d" % c)
-            o_tiles.append(ot)
-            o_views.append(out[r0 : r0 + rows, :].rearrange("(p t) n -> p t n", t=tiles))
-            r0 += rows
+            for t in range(tiles):
+                o_of.append((ot, t, first, tiles))
+            first += tiles
 
         ident_f = const.tile([P, P], F32, name="ident_f")
         make_identity(nc, ident_f[:])
@@ -92,31 +99,18 @@ def tile_fp8columnparallellinear_t_kernel(tc, x, weight, weight_scale_inv, bias,
                 out=w_codes[:].bitcast(FP8X4), scales=w_scales[:], in_=wg[:].rearrange("p n t -> p (n t)")
             )
 
-        units = []
-        for c, tiles in enumerate(CHUNKS):
-            for t0 in range(0, tiles, UNIT):
-                units.append((c, t0))
-        n_units = len(units)
-        store_from = {}
-        for c, tiles in enumerate(CHUNKS):
-            store_from[(c, tiles)] = 0
-        last = len(CHUNKS) - 1
-        store_from[(last, 8)] = 0
-        store_from[(last, 12)] = 8
-        store_from[(last, 16)] = 12
+        n_units = TILES // UNIT
         banks = {}
         grouped = {}
         quant = {}
         sums = {}
 
         def transposes(s):
-            c, t0 = units[s]
-            xf = x_tiles[c][:].bitcast(F32)
             pair = []
             for b in range(2):
                 pt = ps_t.tile([P, 2, 256], F32, name="pt%d_%d" % (s, b), tag="T")
                 for jj in range(2):
-                    t = t0 + 2 * b + jj
+                    xf, t = x_of[UNIT * s + 2 * b + jj]
                     for u in range(2):
                         nc.tensor.transpose(
                             pt[:, u, P * jj : P * jj + P],
@@ -158,11 +152,10 @@ def tile_fp8columnparallellinear_t_kernel(tc, x, weight, weight_scale_inv, bias,
             sums[s] = po
 
         def finish(s):
-            c, t0 = units[s]
-            nc.vector.tensor_tensor(out=o_tiles[c][:, t0 : t0 + UNIT, :], in0=sums[s][:], in1=bias4[:], op=ADD)
-            first = store_from.get((c, t0 + UNIT))
-            if first is not None:
-                nc.sync.dma_start(out=o_views[c][:, first : t0 + UNIT, :], in_=o_tiles[c][:, first : t0 + UNIT, :])
+            ot, t, first, tiles = o_of[UNIT * s]
+            nc.vector.tensor_tensor(out=ot[:, t : t + UNIT, :], in0=sums[s][:], in1=bias4[:], op=ADD)
+            if t + UNIT == tiles:
+                nc.sync.dma_start(out=out_view[:, first : first + tiles, :], in_=ot[:])
 
         for s in range(n_units + 3):
             if s < n_units:

@@ -15,22 +15,24 @@ P = 128
 M, K, N = 16384, 512, 128
 FLOPS = 2 * M * K * N
 
-UNIT = 4
 TILES = M // P
-LOADS = [4, 4, 8, 8, 8, 16, 16, 16, 16, 16, 16]
-STORES = [32, 32, 32, 16, 8, 8]
-BIG = 16
+LOADS = [4,4,8,8,8,16,16,16,16,16,16]
+STORES = [32,32,32,16,8,4,4]
+UNITS = [4,4,8,8,8,8,8,8,8,8,8,8,8,8,8,8,4,4]
+QUAD = 4
 
 
 def tile_fp8columnparallellinear_t_kernel(tc, x, weight, weight_scale_inv, bias, out):
     nc = tc.nc
-    assert sum(LOADS) == TILES and sum(STORES) == TILES
+    BIG = max(LOADS)
+    WIDE = max(UNITS)
+    assert sum(LOADS) == TILES and sum(STORES) == TILES and sum(UNITS) == TILES
     with ExitStack() as ctx:
         const = ctx.enter_context(tc.tile_pool(name="const", bufs=1))
         xpool = ctx.enter_context(tc.tile_pool(name="xin", bufs=1))
         opool = ctx.enter_context(tc.tile_pool(name="res", bufs=1))
-        gpool = ctx.enter_context(tc.tile_pool(name="grouped", bufs=4))
-        qpool = ctx.enter_context(tc.tile_pool(name="quant", bufs=4))
+        gpool = ctx.enter_context(tc.tile_pool(name="grouped", bufs=3))
+        qpool = ctx.enter_context(tc.tile_pool(name="quant", bufs=3))
         ps_t = ctx.enter_context(tc.psum_pool(name="pst", bufs=5))
         ps_o = ctx.enter_context(tc.psum_pool(name="pso", bufs=3))
         ctx.enter_context(tc.manual_schedule())
@@ -72,7 +74,7 @@ def tile_fp8columnparallellinear_t_kernel(tc, x, weight, weight_scale_inv, bias,
         nc.vector.memset(ones[:], 1.0)
         w_codes = const.tile([P, N], U32, name="w_codes", align_bytes=64)
         w_scales = const.tile([P, N], U8, name="w_scales", align_bytes=64)
-        bias4 = const.tile([P, UNIT, N], F32, name="bias4")
+        bias4 = const.tile([P, QUAD, N], F32, name="bias4")
 
         def prepare_weight():
             ps_c = ps_o.tile([P, 256], F32, name="ps_c", tag="O")
@@ -92,80 +94,89 @@ def tile_fp8columnparallellinear_t_kernel(tc, x, weight, weight_scale_inv, bias,
             pw = ps_t.tile([P, 4, P], BF16, name="pw", tag="T")
             for t in range(4):
                 nc.tensor.transpose(pw[:, t, :], wd[:, t, :], ident_b[:])
-            nc.vector.tensor_copy(out=bias4[:], in_=ps_c[:, 0:N].unsqueeze(1).to_broadcast([P, UNIT, N]))
+            nc.vector.tensor_copy(out=bias4[:], in_=ps_c[:, 0:N].unsqueeze(1).to_broadcast([P, QUAD, N]))
             wg = const.tile([P, N, 4], BF16, name="wg", align_bytes=64)
             nc.vector.tensor_copy(out=wg[:], in_=pw[:].rearrange("p t n -> p n t"))
             nc.vector.quantize_mx(
                 out=w_codes[:].bitcast(FP8X4), scales=w_scales[:], in_=wg[:].rearrange("p n t -> p (n t)")
             )
 
-        n_units = TILES // UNIT
+        n_units = len(UNITS)
+        start_of = [sum(UNITS[:s]) for s in range(n_units)]
         banks = {}
         grouped = {}
         quant = {}
         sums = {}
 
         def transposes(s):
-            pair = []
-            for b in range(2):
+            filled = []
+            for b in range(UNITS[s] // 2):
                 pt = ps_t.tile([P, 2, 256], F32, name="pt%d_%d" % (s, b), tag="T")
                 for jj in range(2):
-                    xf, t = x_of[UNIT * s + 2 * b + jj]
+                    xf, t = x_of[start_of[s] + 2 * b + jj]
                     for u in range(2):
                         nc.tensor.transpose(
                             pt[:, u, P * jj : P * jj + P],
                             xf[:, 256 * t + P * u : 256 * t + P * u + P],
                             ident_f[:],
                         )
-                pair.append(pt)
-            banks[s] = pair
+                filled.append(pt)
+            banks[s] = filled
 
         def copies(s):
-            g = gpool.tile([P, UNIT * P * 4], BF16, name="g%d" % s, tag="g", align_bytes=64)
+            g = gpool.tile([P, WIDE * P * 4], BF16, name="g%d" % s, tag="g", align_bytes=64)
             gf = g[:].bitcast(F32)
-            for b in range(2):
+            for b, pt in enumerate(banks[s]):
                 nc.scalar.copy(
                     out=gf[:, 512 * b : 512 * b + 512].rearrange("p (c u) -> p c u", u=2),
-                    in_=banks[s][b][:].rearrange("p u c -> p c u"),
+                    in_=pt[:].rearrange("p u c -> p c u"),
                 )
             grouped[s] = g
 
         def quantise(s):
-            codes = qpool.tile([P, UNIT * P], U32, name="codes%d" % s, tag="codes", align_bytes=64)
-            scales = qpool.tile([P, UNIT * P], U8, name="scales%d" % s, tag="scales", align_bytes=64)
-            nc.vector.quantize_mx(out=codes[:].bitcast(FP8X4), scales=scales[:], in_=grouped[s][:])
+            cols = UNITS[s] * P
+            codes = qpool.tile([P, WIDE * P], U32, name="codes%d" % s, tag="codes", align_bytes=64)
+            scales = qpool.tile([P, WIDE * P], U8, name="scales%d" % s, tag="scales", align_bytes=64)
+            nc.vector.quantize_mx(
+                out=codes[:, 0:cols].bitcast(FP8X4), scales=scales[:, 0:cols], in_=grouped[s][:, 0 : 4 * cols]
+            )
             quant[s] = (codes, scales)
 
         def passes(s):
             codes, scales = quant[s]
-            po = ps_o.tile([P, UNIT, N], F32, name="po%d" % s, tag="O")
-            for j in range(UNIT):
-                nc.tensor.matmul_mx(
-                    out=po[:, j, :],
-                    lhsT=codes[:, P * j : P * j + P].bitcast(FP8X4),
-                    lhsT_scale=scales[:, P * j : P * j + P],
-                    rhs=w_codes[:].bitcast(FP8X4),
-                    rhs_scale=w_scales[:],
-                    start=True,
-                    stop=True,
-                )
-            sums[s] = po
+            filled = []
+            for b in range(UNITS[s] // QUAD):
+                po = ps_o.tile([P, QUAD, N], F32, name="po%d_%d" % (s, b), tag="O")
+                for j in range(QUAD):
+                    col = P * (QUAD * b + j)
+                    nc.tensor.matmul_mx(
+                        out=po[:, j, :],
+                        lhsT=codes[:, col : col + P].bitcast(FP8X4),
+                        lhsT_scale=scales[:, col : col + P],
+                        rhs=w_codes[:].bitcast(FP8X4),
+                        rhs_scale=w_scales[:],
+                        start=True,
+                        stop=True,
+                    )
+                filled.append(po)
+            sums[s] = filled
 
         def finish(s):
-            ot, t, first, tiles = o_of[UNIT * s]
-            nc.vector.tensor_tensor(out=ot[:, t : t + UNIT, :], in0=sums[s][:], in1=bias4[:], op=ADD)
-            if t + UNIT == tiles:
-                nc.sync.dma_start(out=out_view[:, first : first + tiles, :], in_=ot[:])
+            for b, po in enumerate(sums[s]):
+                ot, t, first, tiles = o_of[start_of[s] + QUAD * b]
+                nc.vector.tensor_tensor(out=ot[:, t : t + QUAD, :], in0=po[:], in1=bias4[:], op=ADD)
+                if t + QUAD == tiles:
+                    nc.sync.dma_start(out=out_view[:, first : first + tiles, :], in_=ot[:])
 
-        for s in range(n_units + 3):
+        for s in range(n_units + 2):
+            if 0 <= s - 2:
+                passes(s - 2)
             if s < n_units:
                 transposes(s)
                 copies(s)
             if s == 0:
                 prepare_weight()
-            if 0 <= s - 2 < n_units:
-                passes(s - 2)
             if 0 <= s - 1 < n_units:
                 quantise(s - 1)
-            if 0 <= s - 3 < n_units:
-                finish(s - 3)
+            if 0 <= s - 2:
+                finish(s - 2)

@@ -15,27 +15,24 @@ P = 128
 M, K, N = 16384, 512, 128
 FLOPS = 2 * M * K * N
 
+UNIT = 4
 TILES = M // P
-LOADS = [4,4,8,8,8,16,16,16,16,16,16]
-STORES = [32,32,32,16,8,4,4]
-UNITS = [4,4,8,8,8,8,8,8,8,8,8,8,8,8,8,8,4,4]
-QUAD = 4
+LOADS = [4, 4, 8, 8, 8, 16, 16, 16, 16, 16, 16]
+STORES = [32, 32, 32, 16, 8, 8]
+BIG = 16
 
 
 def tile_fp8columnparallellinear_t_kernel(tc, x, weight, weight_scale_inv, bias, out):
     nc = tc.nc
-    BIG = max(LOADS)
-    WIDE = max(UNITS)
-    assert sum(LOADS) == TILES and sum(STORES) == TILES and sum(UNITS) == TILES
+    assert sum(LOADS) == TILES and sum(STORES) == TILES
     with ExitStack() as ctx:
         const = ctx.enter_context(tc.tile_pool(name="const", bufs=1))
         xpool = ctx.enter_context(tc.tile_pool(name="xin", bufs=1))
         opool = ctx.enter_context(tc.tile_pool(name="res", bufs=1))
-        gpool = ctx.enter_context(tc.tile_pool(name="grouped", bufs=3))
-        qpool = ctx.enter_context(tc.tile_pool(name="quant", bufs=3))
+        gpool = ctx.enter_context(tc.tile_pool(name="grouped", bufs=4))
+        qpool = ctx.enter_context(tc.tile_pool(name="quant", bufs=4))
         ps_t = ctx.enter_context(tc.psum_pool(name="pst", bufs=5))
         ps_o = ctx.enter_context(tc.psum_pool(name="pso", bufs=3))
-        ctx.enter_context(tc.manual_schedule())
 
         w_sb = const.tile([P, K], BF16, name="w_sb")
         row = const.tile([P, 256], BF16, name="row")
@@ -74,7 +71,7 @@ def tile_fp8columnparallellinear_t_kernel(tc, x, weight, weight_scale_inv, bias,
         nc.vector.memset(ones[:], 1.0)
         w_codes = const.tile([P, N], U32, name="w_codes", align_bytes=64)
         w_scales = const.tile([P, N], U8, name="w_scales", align_bytes=64)
-        bias4 = const.tile([P, QUAD, N], F32, name="bias4")
+        bias4 = const.tile([P, UNIT, N], F32, name="bias4")
 
         def prepare_weight():
             ps_c = ps_o.tile([P, 256], F32, name="ps_c", tag="O")
@@ -94,89 +91,80 @@ def tile_fp8columnparallellinear_t_kernel(tc, x, weight, weight_scale_inv, bias,
             pw = ps_t.tile([P, 4, P], BF16, name="pw", tag="T")
             for t in range(4):
                 nc.tensor.transpose(pw[:, t, :], wd[:, t, :], ident_b[:])
-            nc.vector.tensor_copy(out=bias4[:], in_=ps_c[:, 0:N].unsqueeze(1).to_broadcast([P, QUAD, N]))
+            nc.vector.tensor_copy(out=bias4[:], in_=ps_c[:, 0:N].unsqueeze(1).to_broadcast([P, UNIT, N]))
             wg = const.tile([P, N, 4], BF16, name="wg", align_bytes=64)
             nc.vector.tensor_copy(out=wg[:], in_=pw[:].rearrange("p t n -> p n t"))
             nc.vector.quantize_mx(
                 out=w_codes[:].bitcast(FP8X4), scales=w_scales[:], in_=wg[:].rearrange("p n t -> p (n t)")
             )
 
-        n_units = len(UNITS)
-        start_of = [sum(UNITS[:s]) for s in range(n_units)]
+        n_units = TILES // UNIT
         banks = {}
         grouped = {}
         quant = {}
         sums = {}
 
         def transposes(s):
-            filled = []
-            for b in range(UNITS[s] // 2):
+            pair = []
+            for b in range(2):
                 pt = ps_t.tile([P, 2, 256], F32, name="pt%d_%d" % (s, b), tag="T")
                 for jj in range(2):
-                    xf, t = x_of[start_of[s] + 2 * b + jj]
+                    xf, t = x_of[UNIT * s + 2 * b + jj]
                     for u in range(2):
                         nc.tensor.transpose(
                             pt[:, u, P * jj : P * jj + P],
                             xf[:, 256 * t + P * u : 256 * t + P * u + P],
                             ident_f[:],
                         )
-                filled.append(pt)
-            banks[s] = filled
+                pair.append(pt)
+            banks[s] = pair
 
         def copies(s):
-            g = gpool.tile([P, WIDE * P * 4], BF16, name="g%d" % s, tag="g", align_bytes=64)
+            g = gpool.tile([P, UNIT * P * 4], BF16, name="g%d" % s, tag="g", align_bytes=64)
             gf = g[:].bitcast(F32)
-            for b, pt in enumerate(banks[s]):
+            for b in range(2):
                 nc.scalar.copy(
                     out=gf[:, 512 * b : 512 * b + 512].rearrange("p (c u) -> p c u", u=2),
-                    in_=pt[:].rearrange("p u c -> p c u"),
+                    in_=banks[s][b][:].rearrange("p u c -> p c u"),
                 )
             grouped[s] = g
 
         def quantise(s):
-            cols = UNITS[s] * P
-            codes = qpool.tile([P, WIDE * P], U32, name="codes%d" % s, tag="codes", align_bytes=64)
-            scales = qpool.tile([P, WIDE * P], U8, name="scales%d" % s, tag="scales", align_bytes=64)
-            nc.vector.quantize_mx(
-                out=codes[:, 0:cols].bitcast(FP8X4), scales=scales[:, 0:cols], in_=grouped[s][:, 0 : 4 * cols]
-            )
+            codes = qpool.tile([P, UNIT * P], U32, name="codes%d" % s, tag="codes", align_bytes=64)
+            scales = qpool.tile([P, UNIT * P], U8, name="scales%d" % s, tag="scales", align_bytes=64)
+            nc.vector.quantize_mx(out=codes[:].bitcast(FP8X4), scales=scales[:], in_=grouped[s][:])
             quant[s] = (codes, scales)
 
         def passes(s):
             codes, scales = quant[s]
-            filled = []
-            for b in range(UNITS[s] // QUAD):
-                po = ps_o.tile([P, QUAD, N], F32, name="po%d_%d" % (s, b), tag="O")
-                for j in range(QUAD):
-                    col = P * (QUAD * b + j)
-                    nc.tensor.matmul_mx(
-                        out=po[:, j, :],
-                        lhsT=codes[:, col : col + P].bitcast(FP8X4),
-                        lhsT_scale=scales[:, col : col + P],
-                        rhs=w_codes[:].bitcast(FP8X4),
-                        rhs_scale=w_scales[:],
-                        start=True,
-                        stop=True,
-                    )
-                filled.append(po)
-            sums[s] = filled
+            po = ps_o.tile([P, UNIT, N], F32, name="po%d" % s, tag="O")
+            for j in range(UNIT):
+                nc.tensor.matmul_mx(
+                    out=po[:, j, :],
+                    lhsT=codes[:, P * j : P * j + P].bitcast(FP8X4),
+                    lhsT_scale=scales[:, P * j : P * j + P],
+                    rhs=w_codes[:].bitcast(FP8X4),
+                    rhs_scale=w_scales[:],
+                    start=True,
+                    stop=True,
+                )
+            sums[s] = po
 
         def finish(s):
-            for b, po in enumerate(sums[s]):
-                ot, t, first, tiles = o_of[start_of[s] + QUAD * b]
-                nc.vector.tensor_tensor(out=ot[:, t : t + QUAD, :], in0=po[:], in1=bias4[:], op=ADD)
-                if t + QUAD == tiles:
-                    nc.sync.dma_start(out=out_view[:, first : first + tiles, :], in_=ot[:])
+            ot, t, first, tiles = o_of[UNIT * s]
+            nc.vector.tensor_tensor(out=ot[:, t : t + UNIT, :], in0=sums[s][:], in1=bias4[:], op=ADD)
+            if t + UNIT == tiles:
+                nc.sync.dma_start(out=out_view[:, first : first + tiles, :], in_=ot[:])
 
-        for s in range(n_units + 2):
-            if 0 <= s - 2:
-                passes(s - 2)
+        for s in range(n_units + 3):
             if s < n_units:
                 transposes(s)
                 copies(s)
             if s == 0:
                 prepare_weight()
+            if 0 <= s - 2 < n_units:
+                passes(s - 2)
             if 0 <= s - 1 < n_units:
                 quantise(s - 1)
-            if 0 <= s - 2:
-                finish(s - 2)
+            if 0 <= s - 3 < n_units:
+                finish(s - 3)

from contextlib import ExitStack

import concourse.mybir as mybir
from concourse.masks import make_identity

F32 = mybir.dt.float32
BF16 = mybir.dt.bfloat16
U32 = mybir.dt.uint32
U8 = mybir.dt.uint8
FP8X4 = mybir.dt.float8_e4m3fn_x4
MULT = mybir.AluOpType.mult
ADD = mybir.AluOpType.add

P = 128
M, K, N = 16384, 512, 128
FLOPS = 2 * M * K * N

UNIT = 4
TILES = M // P
LOADS = [4, 4, 8, 8, 8, 16, 16, 16, 16, 16, 16]
STORES = [32, 32, 32, 16, 8, 8]
BIG = 16


def tile_fp8columnparallellinear_t_kernel(tc, x, weight, weight_scale_inv, bias, out):
    nc = tc.nc
    assert sum(LOADS) == TILES and sum(STORES) == TILES
    with ExitStack() as ctx:
        const = ctx.enter_context(tc.tile_pool(name="const", bufs=1))
        xpool = ctx.enter_context(tc.tile_pool(name="xin", bufs=1))
        opool = ctx.enter_context(tc.tile_pool(name="res", bufs=1))
        gpool = ctx.enter_context(tc.tile_pool(name="grouped", bufs=4))
        qpool = ctx.enter_context(tc.tile_pool(name="quant", bufs=4))
        ps_t = ctx.enter_context(tc.psum_pool(name="pst", bufs=5))
        ps_o = ctx.enter_context(tc.psum_pool(name="pso", bufs=3))

        w_sb = const.tile([P, K], BF16, name="w_sb")
        row = const.tile([P, 256], BF16, name="row")
        nc.vector.memset(row[:], 0.0)
        x_view = x.rearrange("(p t) k -> p t k", t=TILES)
        out_view = out.rearrange("(p t) n -> p t n", t=TILES)
        x_of = []
        first = 0
        for c, tiles in enumerate(LOADS):
            if tiles == BIG:
                xt = xpool.tile([P, tiles, K], BF16, name="xbig%d" % c, tag="xbig", bufs=5)
            else:
                xt = xpool.tile([P, tiles, K], BF16, name="xsmall%d" % c)
            nc.sync.dma_start(out=xt[:], in_=x_view[:, first : first + tiles, :])
            if c == 0:
                nc.sync.dma_start(out=w_sb[:], in_=weight)
                nc.sync.dma_start(out=row[0:1, 0:N], in_=bias.rearrange("(o n) -> o n", o=1))
                nc.sync.dma_start(out=row[0:1, N : N + 4], in_=weight_scale_inv)
            xf = xt[:].rearrange("p t k -> p (t k)").bitcast(F32)
            for t in range(tiles):
                x_of.append((xf, t))
            first += tiles
        o_of = []
        first = 0
        for c, tiles in enumerate(STORES):
            ot = opool.tile([P, tiles, N], F32, name="o%d" % c)
            for t in range(tiles):
                o_of.append((ot, t, first, tiles))
            first += tiles

        ident_f = const.tile([P, P], F32, name="ident_f")
        make_identity(nc, ident_f[:])
        ident_b = const.tile([P, P], BF16, name="ident_b")
        make_identity(nc, ident_b[:])
        ones = const.tile([P, P], BF16, name="ones")
        nc.vector.memset(ones[:], 1.0)
        w_codes = const.tile([P, N], U32, name="w_codes", align_bytes=64)
        w_scales = const.tile([P, N], U8, name="w_scales", align_bytes=64)
        bias4 = const.tile([P, UNIT, N], F32, name="bias4")

        def prepare_weight():
            ps_c = ps_o.tile([P, 256], F32, name="ps_c", tag="O")
            nc.tensor.matmul(out=ps_c[:], lhsT=ones[:], rhs=row[:], start=True, stop=True)
            scale_sb = const.tile([P, 4], F32, name="scale_sb")
            nc.vector.tensor_copy(out=scale_sb[:], in_=ps_c[:, N : N + 4])
            wd = const.tile([P, 4, P], BF16, name="wd")
            for j in range(4):
                u, h = divmod(j, 2)
                nc.vector.tensor_scalar(
                    out=wd[:, 2 * u : 2 * u + 2, 64 * h : 64 * h + 64],
                    in0=w_sb[:, P * j : P * j + P].rearrange("n (q e) -> n e q", e=2),
                    scalar1=scale_sb[:, j : j + 1],
                    scalar2=None,
                    op0=MULT,
                )
            pw = ps_t.tile([P, 4, P], BF16, name="pw", tag="T")
            for t in range(4):
                nc.tensor.transpose(pw[:, t, :], wd[:, t, :], ident_b[:])
            nc.vector.tensor_copy(out=bias4[:], in_=ps_c[:, 0:N].unsqueeze(1).to_broadcast([P, UNIT, N]))
            wg = const.tile([P, N, 4], BF16, name="wg", align_bytes=64)
            nc.vector.tensor_copy(out=wg[:], in_=pw[:].rearrange("p t n -> p n t"))
            nc.vector.quantize_mx(
                out=w_codes[:].bitcast(FP8X4), scales=w_scales[:], in_=wg[:].rearrange("p n t -> p (n t)")
            )

        n_units = TILES // UNIT
        banks = {}
        grouped = {}
        quant = {}
        sums = {}

        def transposes(s):
            pair = []
            for b in range(2):
                pt = ps_t.tile([P, 2, 256], F32, name="pt%d_%d" % (s, b), tag="T")
                for jj in range(2):
                    xf, t = x_of[UNIT * s + 2 * b + jj]
                    for u in range(2):
                        nc.tensor.transpose(
                            pt[:, u, P * jj : P * jj + P],
                            xf[:, 256 * t + P * u : 256 * t + P * u + P],
                            ident_f[:],
                        )
                pair.append(pt)
            banks[s] = pair

        def copies(s):
            g = gpool.tile([P, UNIT * P * 4], BF16, name="g%d" % s, tag="g", align_bytes=64)
            gf = g[:].bitcast(F32)
            for b in range(2):
                nc.scalar.copy(
                    out=gf[:, 512 * b : 512 * b + 512].rearrange("p (c u) -> p c u", u=2),
                    in_=banks[s][b][:].rearrange("p u c -> p c u"),
                )
            grouped[s] = g

        def quantise(s):
            codes = qpool.tile([P, UNIT * P], U32, name="codes%d" % s, tag="codes", align_bytes=64)
            scales = qpool.tile([P, UNIT * P], U8, name="scales%d" % s, tag="scales", align_bytes=64)
            nc.vector.quantize_mx(out=codes[:].bitcast(FP8X4), scales=scales[:], in_=grouped[s][:])
            quant[s] = (codes, scales)

        def passes(s):
            codes, scales = quant[s]
            po = ps_o.tile([P, UNIT, N], F32, name="po%d" % s, tag="O")
            for j in range(UNIT):
                nc.tensor.matmul_mx(
                    out=po[:, j, :],
                    lhsT=codes[:, P * j : P * j + P].bitcast(FP8X4),
                    lhsT_scale=scales[:, P * j : P * j + P],
                    rhs=w_codes[:].bitcast(FP8X4),
                    rhs_scale=w_scales[:],
                    start=True,
                    stop=True,
                )
            sums[s] = po

        def finish(s):
            ot, t, first, tiles = o_of[UNIT * s]
            nc.vector.tensor_tensor(out=ot[:, t : t + UNIT, :], in0=sums[s][:], in1=bias4[:], op=ADD)
            if t + UNIT == tiles:
                nc.sync.dma_start(out=out_view[:, first : first + tiles, :], in_=ot[:])

        for s in range(n_units + 3):
            if s < n_units:
                transposes(s)
                copies(s)
            if s == 0:
                prepare_weight()
            if 0 <= s - 2 < n_units:
                passes(s - 2)
            if 0 <= s - 1 < n_units:
                quantise(s - 1)
            if 0 <= s - 3 < n_units:
                finish(s - 3)
